import numpy as np
import ml_dtypes


BF16 = ml_dtypes.bfloat16


def bf(x):
    return np.asarray(x, np.float32).astype(BF16)


def f64(x):
    return np.asarray(x).astype(np.float64)


E2M1 = np.array([0.0, 0.5, 1.0, 1.5, 2.0, 3.0, 4.0, 6.0, -0.0, -0.5, -1.0, -1.5, -2.0, -3.0, -4.0, -6.0])


def pack_weight(w, fmt):
    k, n = w.shape
    w = f64(bf(w)).reshape(k // 32, 32, n)
    amax = np.abs(w).max(1)
    if fmt == "e4m3":
        byte = np.frexp(amax)[1] - 1 + 127 - 7
    else:
        mant, ex = np.frexp(amax / 6.0)
        byte = np.where(mant > 0.5, ex, ex - 1) + 127
    byte = np.clip(np.where(amax > 0, byte, 1), 1, 254)
    scaled = (w * np.exp2(127.0 - byte)[:, None, :]).reshape(k, n).astype(np.float32)
    by_word = np.ascontiguousarray(scaled.reshape(k // 512, 128, 4, n).transpose(0, 1, 3, 2))
    if fmt == "e4m3":
        words = by_word.astype(ml_dtypes.float8_e4m3fn).view(np.uint8)
    else:
        c = by_word.astype(ml_dtypes.float4_e2m1fn).view(np.uint8) & 0xF
        words = c[..., 0::2] | (c[..., 1::2] << 4)
    return np.ascontiguousarray(words), np.ascontiguousarray(byte.astype(np.uint8).reshape(k // 512, 16, n))


def unpack_weight(words, scales, fmt):
    g, p, n, _ = words.shape
    if fmt == "e4m3":
        vals = np.ascontiguousarray(words).view(ml_dtypes.float8_e4m3fn).astype(np.float64)
    else:
        nib = np.empty((g, p, n, 4), np.uint8)
        nib[..., 0::2] = words & 0xF
        nib[..., 1::2] = words >> 4
        vals = E2M1[nib]
    vals = vals * np.repeat(np.exp2(scales.astype(np.float64) - 127.0), 8, axis=1)[..., None]
    return vals.transpose(0, 1, 3, 2).reshape(g * 512, n)

def pack4(w):
    words, scales = pack_weight(w, "e2m1")
    return words.reshape(words.shape[0], 128, -1), scales


def unpack4(words, scales):
    return unpack_weight(words.reshape(words.shape[0], 128, -1, 2), scales, "e2m1")


def kspread(k):
    return np.exp2(np.repeat(np.random.randint(-6, 7, k // 32), 32).astype(np.float64))


B, S, HID, NH, HD, RD, RATIO = 1, 2048, 4096, 8, 128, 64, 4
THETA = 10000.0
NW = S // RATIO
HALF = RD // 2


def rope_tables(positions):
    inv_freq = 1.0 / THETA ** (np.arange(HALF) / HALF)
    ang = positions[:, None] * inv_freq[None, :]
    return np.cos(ang), np.sin(ang)


def rope_interleaved(x, cos, sin):
    nope, rope = x[..., :-RD], x[..., -RD:]
    pr = rope.reshape(rope.shape[:-1] + (HALF, 2))
    a, b = pr[..., 0], pr[..., 1]
    new = np.stack([a * cos - b * sin, a * sin + b * cos], axis=-1).reshape(rope.shape)
    return np.concatenate([nope, new], axis=-1)


def remap(t, fill):
    cur = t[..., HD:]
    prev = np.concatenate([np.full((B, 1, RATIO, HD), fill), t[:, :-1, :, :HD]], axis=1)
    return np.concatenate([prev, cur], axis=2)


def pool_overlap(kv, gate, ape):
    kv_o = remap(kv.reshape(B, NW, RATIO, 2 * HD), 0.0)
    gate_o = remap(gate.reshape(B, NW, RATIO, 2 * HD) + ape, -np.inf)
    e = np.exp(gate_o - gate_o.max(axis=2, keepdims=True))
    w = e / e.sum(axis=2, keepdims=True)
    return (kv_o * w).sum(axis=2)


def setup_inputs():
    s = kspread(HID)
    hidden = np.random.standard_normal((B, S, HID)) * s
    hidden_words, hidden_scales = pack4(hidden.reshape(B * S, HID).T)
    wkv_words, wkv_scales = pack4(np.random.standard_normal((HID, 2 * HD)) * 2.0 / np.sqrt(HID) / s[:, None])
    wgate_words, wgate_scales = pack4(np.random.standard_normal((HID, 2 * HD)) / np.sqrt(HID) / s[:, None])
    ape = bf(np.random.standard_normal((RATIO, 2 * HD)) * 0.5)
    return {"hidden_words": hidden_words, "hidden_scales": hidden_scales,
            "wkv_words": wkv_words, "wkv_scales": wkv_scales,
            "wgate_words": wgate_words, "wgate_scales": wgate_scales,
            "ape": ape}


def reference(hidden_words, hidden_scales, wkv_words, wkv_scales, wgate_words, wgate_scales, ape):
    hq = unpack4(hidden_words, hidden_scales).T.reshape(B, S, HID)
    kv = hq @ unpack4(wkv_words, wkv_scales)
    gate = hq @ unpack4(wgate_words, wgate_scales)
    pooled = pool_overlap(kv, gate, f64(ape))
    ck, sk = rope_tables(np.arange(NW) * RATIO)
    k_rot = rope_interleaved(pooled, ck, sk)
    return k_rot, pooled

@@ -1,0 +1,314 @@
+from contextlib import ExitStack
+import concourse.mybir as mybir
+from concourse.masks import make_identity
+
+FLOPS = 2 * 2048 * 4096 * 512
+
+F32 = mybir.dt.float32
+BF16 = mybir.dt.bfloat16
+I32 = mybir.dt.int32
+U8 = mybir.dt.uint8
+FP4 = mybir.dt.float4_e2m1fn_x4
+ALU = mybir.AluOpType
+ACT = mybir.ActivationFunctionType
+AX = mybir.AxisListType
+
+P = 128
+PASSES = 8
+BLOCKS = 4
+BLOCK = 512
+WIN = 128
+RATIO = 4
+HALF = 32
+THETA = 10000.0
+PITCH = 132
+NEG = -1.0e30
+HI_STEPS = 32768.0
+TWO_PI = 6.283185307179586
+
+LOADS = (
+    ("s", "h0", 0, 2), ("s", "wg", 0, 8), ("c", "h0", 0, 2), ("c", "wg", 0, 2),
+    ("s", "h0", 2, 8), ("c", "h0", 2, 4), ("c", "wg", 2, 8), ("c", "h0", 4, 8),
+    ("s", "h1", 0, 8), ("c", "h1", 0, 4), ("c", "h1", 4, 8),
+    ("s", "h2", 0, 8), ("c", "h2", 0, 4), ("c", "h2", 4, 8),
+    ("s", "h3", 0, 8), ("c", "h3", 0, 4), ("c", "h3", 4, 8),
+    ("s", "wk", 0, 8), ("c", "wk", 0, 8),
+)
+LAST_PIECES = ((0, 64), (64, 32), (96, 32))
+
+
+def tile_deepseekv4attention_pa_kernel(
+    tc, hidden_words, hidden_scales, wkv_words, wkv_scales, wgate_words, wgate_scales, ape, out_0, out_1
+):
+    nc = tc.nc
+    with ExitStack() as ctx:
+        keep = ctx.enter_context(tc.tile_pool(name="keep", bufs=1))
+        work = ctx.enter_context(tc.tile_pool(name="work", bufs=2))
+        acc_pool = ctx.enter_context(tc.psum_pool(name="acc", bufs=6))
+        tp_pool = ctx.enter_context(tc.psum_pool(name="tp", bufs=2))
+        ctx.enter_context(tc.manual_schedule())
+
+        source = {"wg": (wgate_words, wgate_scales, 0, 256), "wk": (wkv_words, wkv_scales, 0, 256)}
+        for b in range(BLOCKS):
+            source["h%d" % b] = (hidden_words, hidden_scales, BLOCK * b, BLOCK)
+        codes = {}
+        planes = {}
+
+        ape_rows = keep.tile([2 * RATIO, P], BF16, name="ape_rows")
+        nc.gpsimd.dma_start(out=ape_rows[:], in_=ape.rearrange("r (h f) -> (r h) f", h=2))
+
+        plane_tiles = {}
+        for kind, name, g0, g1 in LOADS:
+            if kind == "s":
+                cols = source[name][3]
+                t = keep.tile([P, g1 - g0, cols], U8, name="%s_s%d" % (name, g0), align_bytes=64)
+                nc.vector.memset(t[:].bitcast(I32), 0)
+                plane_tiles[(name, g0)] = t
+                for g in range(g0, g1):
+                    planes[(name, g)] = t[:, g - g0, :]
+        for kind, name, g0, g1 in LOADS:
+            words, scales, c0, cols = source[name]
+            if kind == "s":
+                t = plane_tiles[(name, g0)]
+                for q in range(4):
+                    nc.sync.dma_start(
+                        out=t[32 * q : 32 * q + 4, :, :].bitcast(I32),
+                        in_=scales[g0:g1, 4 * q : 4 * q + 4, c0 : c0 + cols].rearrange("g r n -> r g n").bitcast(I32),
+                    )
+            else:
+                t = keep.tile([P, g1 - g0, 2 * cols], U8, name="%s_c%d" % (name, g0), align_bytes=64)
+                nc.sync.dma_start(
+                    out=t[:].bitcast(I32),
+                    in_=words[g0:g1, :, 2 * c0 : 2 * (c0 + cols)].rearrange("g p n -> p g n").bitcast(I32),
+                )
+                for g in range(g0, g1):
+                    codes[(name, g)] = t[:, g - g0, :]
+
+        zero = keep.tile([P, 1], F32, name="zero")
+        nc.gpsimd.memset(zero[:], 0.0)
+        wcol = keep.tile([P, BLOCKS], F32, name="wcol")
+        nc.gpsimd.iota(wcol[:], pattern=[[WIN, BLOCKS]], base=0, channel_multiplier=1, allow_small_or_imprecise_dtypes=True)
+        ape_pad = keep.tile([P, P], F32, name="ape_pad")
+        nc.gpsimd.memset(ape_pad[:], 0.0)
+        ident = keep.tile([P, P], F32, name="ident")
+        make_identity(nc, ident[:])
+
+        xg = [keep.tile([P, 2 * RATIO, PITCH], F32, name="xg%d" % b) for b in range(BLOCKS)]
+        carry = [keep.tile([P, 1, RATIO], F32, name="carry%d" % b) for b in range(BLOCKS)]
+        ex = [keep.tile([P, WIN, 2 * RATIO], F32, name="ex%d" % b) for b in range(BLOCKS)]
+        nc.gpsimd.memset(xg[0][:, 0:RATIO, 0:1], NEG)
+        nc.gpsimd.memset(carry[0][:], 0.0)
+
+        scrap = keep.tile([P, 1], F32, name="scrap")
+        nc.scalar.activation(out=scrap[:], in_=zero[:], func=ACT.Sin)
+        turn_hi = keep.tile([P, BLOCKS, HALF], F32, name="turn_hi")
+        turn_lo = keep.tile([P, BLOCKS, HALF], F32, name="turn_lo")
+        steps = [RATIO * THETA ** (-j / HALF) / TWO_PI for j in range(HALF)]
+        for j in range(HALF):
+            nc.scalar.mul(out=turn_hi[:, :, j], in_=wcol[:], mul=round(steps[j] * HI_STEPS) / HI_STEPS)
+        for j in range(HALF):
+            nc.scalar.mul(out=turn_lo[:, :, j], in_=wcol[:], mul=steps[j] - round(steps[j] * HI_STEPS) / HI_STEPS)
+
+        nc.vector.tensor_copy(out=ape_pad[0 : 2 * RATIO, :], in_=ape_rows[:])
+        ape_ps = tp_pool.tile([P, P], F32, name="ape_ps", tag="tp")
+        nc.tensor.transpose(out=ape_ps[:], in_=ape_pad[:], identity=ident[:])
+        ape_t = keep.tile([P, 2 * RATIO], F32, name="ape_t")
+        nc.scalar.copy(out=ape_t[:], in_=ape_ps[:, 0 : 2 * RATIO])
+
+        whole = keep.tile([P, BLOCKS, HALF], I32, name="whole")
+        nc.vector.tensor_copy(out=whole[:], in_=turn_hi[:])
+        frac = keep.tile([P, 2, BLOCKS, HALF], F32, name="frac")
+        nc.vector.tensor_tensor(out=frac[:, 0], in0=turn_hi[:], in1=whole[:], op=ALU.subtract)
+        nc.vector.tensor_tensor(out=frac[:, 0], in0=frac[:, 0], in1=turn_lo[:], op=ALU.add)
+        nc.vector.tensor_scalar_add(out=frac[:, 1], in0=frac[:, 0], scalar1=0.25)
+        wrap1 = keep.tile([P, 2 * BLOCKS * HALF], F32, name="wrap1")
+        wrap2 = keep.tile([P, 2 * BLOCKS * HALF], F32, name="wrap2")
+        flat = frac[:].rearrange("p a c j -> p (a c j)")
+        nc.vector.scalar_tensor_tensor(out=wrap1[:], in0=flat, scalar=0.5, in1=flat, op0=ALU.is_gt, op1=ALU.subtract)
+        nc.vector.scalar_tensor_tensor(out=wrap2[:], in0=wrap1[:], scalar=0.5, in1=wrap1[:], op0=ALU.is_gt, op1=ALU.subtract)
+        sincos = keep.tile([P, 2, BLOCKS, HALF], F32, name="sincos")
+        nc.scalar.activation(out=sincos[:].rearrange("p a c j -> p (a c j)"), in_=wrap2[:], func=ACT.Sin, scale=TWO_PI)
+
+        def mx(acc, wname, half, b, g, col0, ncol):
+            nc.tensor.matmul_mx(
+                out=acc,
+                lhsT=codes[(wname, g)][:, 256 * half : 256 * half + 256].bitcast(FP4),
+                lhsT_scale=planes[(wname, g)][:, P * half : P * half + P],
+                rhs=codes[("h%d" % b, g)][:, 2 * col0 : 2 * (col0 + ncol)].bitcast(FP4),
+                rhs_scale=planes[("h%d" % b, g)][:, col0 : col0 + ncol],
+                start=(g == 0),
+                stop=(g == PASSES - 1),
+            )
+
+        def gate_matmuls(b):
+            lo = acc_pool.tile([P, BLOCK], F32, name="gate_lo%d" % b, tag="acc")
+            hi = acc_pool.tile([P, BLOCK], F32, name="gate_hi%d" % b, tag="acc")
+            for g in range(PASSES):
+                mx(lo[:], "wg", 0, b, g, 0, BLOCK)
+                mx(hi[:], "wg", 1, b, g, 0, BLOCK)
+            return lo, hi
+
+        def add_offsets(b, banks):
+            for half in range(2):
+                shift = 1 - half
+                for r in range(RATIO):
+                    nc.scalar.activation(
+                        out=xg[b][:, RATIO * half + r, shift : shift + WIN],
+                        in_=banks[half][:, r:BLOCK:RATIO],
+                        func=ACT.Identity,
+                        bias=ape_t[:, 2 * r + half : 2 * r + half + 1],
+                        scale=1.0,
+                    )
+            if b + 1 < BLOCKS:
+                nc.gpsimd.tensor_copy(out=xg[b + 1][:, 0:RATIO, 0:1], in_=xg[b][:, 0:RATIO, WIN : WIN + 1])
+
+        tt = nc.vector.tensor_tensor
+        below = {}
+
+        def max_steps(b):
+            m4 = work.tile([P, 4, WIN], F32, name="m4")
+            m2 = work.tile([P, 2, WIN], F32, name="m2")
+            m1 = work.tile([P, WIN], F32, name="m1")
+            dm = work.tile([P, 8, WIN], F32, name="dm")
+            below[b] = dm
+            return [
+                lambda: tt(out=m4[:], in0=xg[b][:, 0:4, 0:WIN], in1=xg[b][:, 4:8, 0:WIN], op=ALU.max),
+                lambda: tt(out=m2[:], in0=m4[:, 0:2, :], in1=m4[:, 2:4, :], op=ALU.max),
+                lambda: tt(out=m1[:], in0=m2[:, 0, :], in1=m2[:, 1, :], op=ALU.max),
+                lambda: tt(out=dm[:], in0=xg[b][:, :, 0:WIN], in1=m1[:].unsqueeze(1).to_broadcast([P, 8, WIN]), op=ALU.subtract),
+            ]
+
+        def exponent(b):
+            for half in range(2):
+                s = slice(RATIO * half, RATIO * half + RATIO)
+                nc.scalar.activation(out=ex[b][:, :, s], in_=below[b][:, s, :].rearrange("p s w -> p w s"), func=ACT.Exp)
+
+        denom = keep.tile([P, BLOCKS, WIN], F32, name="denom")
+
+        def sum_steps(b, parts):
+            def one(w0, w1):
+                return lambda: nc.vector.tensor_reduce(out=denom[:, b, w0:w1], in_=ex[b][:, w0:w1, :], axis=AX.X, op=ALU.add)
+            return [one(w0, w1) for w0, w1 in parts]
+
+        log_d = keep.tile([P, BLOCKS, WIN], F32, name="log_d")
+        recip = keep.tile([P, BLOCKS, WIN], F32, name="recip")
+
+        def reciprocals():
+            nc.scalar.activation(out=log_d[:], in_=denom[:], func=ACT.Ln)
+            nc.scalar.activation(out=recip[:], in_=log_d[:], func=ACT.Exp, scale=-1.0)
+
+        def kv_matmuls(b, half, w0, nw):
+            acc = acc_pool.tile([P, RATIO * nw], F32, name="kv%d_%d_%d" % (half, b, w0), tag="acc")
+            for g in range(PASSES):
+                mx(acc[:], "wk", half, b, g, RATIO * w0, RATIO * nw)
+            return acc
+
+        pooled_t = [keep.tile([P, WIN], F32, name="pooled_t%d" % b) for b in range(BLOCKS)]
+        prod = [keep.tile([P, WIN, 2 * RATIO], F32, name="prod%d" % b) for b in range(BLOCKS)]
+        LAST = BLOCKS - 1
+
+        def lo_steps(b, acc):
+            out = [
+                lambda: tt(out=prod[b][:, 1:WIN, 0:4], in0=acc[:, 0 : BLOCK - RATIO].rearrange("p (w r) -> p w r", r=RATIO), in1=ex[b][:, 1:WIN, 0:4], op=ALU.mult),
+                lambda: tt(out=prod[b][:, 0:1, 0:4], in0=carry[b][:], in1=ex[b][:, 0:1, 0:4], op=ALU.mult),
+            ]
+            if b < LAST:
+                out.append(lambda: nc.vector.tensor_copy(out=carry[b + 1][:, 0, :], in_=acc[:, BLOCK - RATIO : BLOCK]))
+            return out
+
+        def hi_steps(b, w0, nw, acc):
+            cols = slice(w0, w0 + nw)
+            total = pooled_t[b] if b == LAST else work.tile([P, WIN], F32, name="total")
+            out = [
+                lambda: tt(out=prod[b][:, cols, 4:8], in0=acc[:].rearrange("p (w r) -> p w r", r=RATIO), in1=ex[b][:, cols, 4:8], op=ALU.mult),
+                lambda: nc.vector.tensor_reduce(out=total[:, cols], in_=prod[b][:, cols, :], axis=AX.X, op=ALU.add),
+            ]
+            if b < LAST:
+                out.append(lambda: tt(out=pooled_t[b][:, cols], in0=total[:, cols], in1=recip[:, b, cols], op=ALU.mult))
+            return out
+
+        def prescale():
+            tt(out=ex[LAST][:], in0=ex[LAST][:], in1=recip[:, LAST, :].unsqueeze(2).to_broadcast([P, WIN, 8]), op=ALU.mult)
+
+        pooled = [keep.tile([P, P], F32, name="pooled%d" % b) for b in range(BLOCKS)]
+        turned = [keep.tile([P, HALF, 2], F32, name="turned%d" % b) for b in range(BLOCKS)]
+        rope_in = {}
+
+        def turn_round(b, twice):
+            ps = tp_pool.tile([P, P], F32, name="pooled_ps%d" % b, tag="tp")
+            nc.tensor.transpose(out=ps[:], in_=pooled_t[b][:], identity=ident[:])
+            rope_in[b] = pooled[b]
+            if twice:
+                ps2 = tp_pool.tile([P, P], F32, name="pooled_pt%d" % b, tag="tp")
+                nc.tensor.transpose(out=ps2[:], in_=pooled_t[b][:], identity=ident[:])
+                rope_in[b] = ps2
+            nc.scalar.copy(out=pooled[b][:], in_=ps[:])
+            rows = slice(WIN * b, WIN * (b + 1))
+            nc.sync.dma_start(out=out_1[0, rows, :], in_=pooled[b][:])
+            nc.sync.dma_start(out=out_0[0, rows, 0:64], in_=pooled[b][:, 0:64])
+
+        def rope_steps(b):
+            pairs = rope_in[b][:, 64:128].rearrange("p (j e) -> p j e", e=2)
+            by_cos = work.tile([P, HALF, 2], F32, name="by_cos")
+            by_sin = work.tile([P, HALF, 2], F32, name="by_sin")
+            cos = sincos[:, 1, b, :].unsqueeze(2).to_broadcast([P, HALF, 2])
+            sin = sincos[:, 0, b, :].unsqueeze(2).to_broadcast([P, HALF, 2])
+            rows = slice(WIN * b, WIN * (b + 1))
+            return [
+                lambda: tt(out=by_cos[:], in0=pairs, in1=cos, op=ALU.mult),
+                lambda: tt(out=by_sin[:], in0=pairs, in1=sin, op=ALU.mult),
+                lambda: tt(out=turned[b][:, :, 0], in0=by_cos[:, :, 0], in1=by_sin[:, :, 1], op=ALU.subtract),
+                lambda: tt(out=turned[b][:, :, 1], in0=by_cos[:, :, 1], in1=by_sin[:, :, 0], op=ALU.add),
+                lambda: nc.sync.dma_start(out=out_0[0, rows, 64:128], in_=turned[b][:].rearrange("p j e -> p (j e)")),
+            ]
+
+        def run(*lists):
+            for steps_ in lists:
+                for step in steps_:
+                    step()
+
+        def weave(a, c):
+            for i in range(max(len(a), len(c))):
+                run(a[i : i + 1], c[i : i + 1])
+
+        THIRDS = ((0, 48), (48, 96), (96, 128))
+        WHOLE = ((0, WIN),)
+
+        for b in range(BLOCKS):
+            banks = gate_matmuls(b)
+            add_offsets(b, banks)
+            if b == 0:
+                nc.scalar.activation(out=scrap[:], in_=zero[:], func=ACT.Exp)
+            else:
+                exponent(b - 1)
+            weave(max_steps(b), sum_steps(b - 2, THIRDS) if b >= 2 else [])
+
+        late = []
+        for b in range(BLOCKS):
+            lo_acc = kv_matmuls(b, 0, 0, WIN)
+            if b == 0:
+                exponent(LAST)
+                run(sum_steps(LAST - 1, WHOLE))
+            run(lo_steps(b, lo_acc))
+            if b < LAST:
+                acc = kv_matmuls(b, 1, 0, WIN)
+                his = hi_steps(b, 0, WIN, acc)
+                if b == 0:
+                    run(his[0:1], sum_steps(LAST, WHOLE), his[1:2])
+                    reciprocals()
+                    late = late + his[2:3]
+                elif b == 1:
+                    run(his[0:2], late, his[2:3])
+                    prescale()
+                else:
+                    run(his)
+                    turn_round(0, False)
+                    turn_round(1, False)
+                    weave(rope_steps(0), rope_steps(1))
+            else:
+                accs = [kv_matmuls(b, 1, w0, nw) for w0, nw in LAST_PIECES]
+                his = [hi_steps(b, w0, nw, acc) for (w0, nw), acc in zip(LAST_PIECES, accs)]
+                run(his[0][0:1], his[1][0:1], his[0][1:2], his[2][0:1], his[1][1:2], his[2][1:2])
+        turn_round(2, False)
+        turn_round(3, True)
+        run(rope_steps(2), rope_steps(3))

@@ -35,6 +35,7 @@ LOADS = (
     ("s", "wk", 0, 8), ("c", "wk", 0, 8),
 )
 LAST_PIECES = ((0, 64), (64, 32), (96, 32))
+PRE = 64
 
 
 def tile_deepseekv4attention_pa_kernel(
@@ -94,10 +95,10 @@ def tile_deepseekv4attention_pa_kernel(
         make_identity(nc, ident[:])
 
         xg = [keep.tile([P, 2 * RATIO, PITCH], F32, name="xg%d" % b) for b in range(BLOCKS)]
-        carry = [keep.tile([P, 1, RATIO], F32, name="carry%d" % b) for b in range(BLOCKS)]
-        ex = [keep.tile([P, WIN, 2 * RATIO], F32, name="ex%d" % b) for b in range(BLOCKS)]
+        ex_all = keep.tile([P, BLOCKS * WIN, 2 * RATIO], F32, name="ex_all")
+        prod_all = keep.tile([P, BLOCKS * WIN, 2 * RATIO], F32, name="prod_all")
         nc.gpsimd.memset(xg[0][:, 0:RATIO, 0:1], NEG)
-        nc.gpsimd.memset(carry[0][:], 0.0)
+        nc.vector.memset(prod_all[:, 0:1, 0:RATIO], 0.0)
 
         scrap = keep.tile([P, 1], F32, name="scrap")
         nc.scalar.activation(out=scrap[:], in_=zero[:], func=ACT.Sin)
@@ -181,13 +182,13 @@ def tile_deepseekv4attention_pa_kernel(
         def exponent(b):
             for half in range(2):
                 s = slice(RATIO * half, RATIO * half + RATIO)
-                nc.scalar.activation(out=ex[b][:, :, s], in_=below[b][:, s, :].rearrange("p s w -> p w s"), func=ACT.Exp)
+                nc.scalar.activation(out=ex_all[:, WIN * b : WIN * (b + 1), s], in_=below[b][:, s, :].rearrange("p s w -> p w s"), func=ACT.Exp)
 
         denom = keep.tile([P, BLOCKS, WIN], F32, name="denom")
 
         def sum_steps(b, parts):
             def one(w0, w1):
-                return lambda: nc.vector.tensor_reduce(out=denom[:, b, w0:w1], in_=ex[b][:, w0:w1, :], axis=AX.X, op=ALU.add)
+                return lambda: nc.vector.tensor_reduce(out=denom[:, b, w0:w1], in_=ex_all[:, WIN * b + w0 : WIN * b + w1, :], axis=AX.X, op=ALU.add)
             return [one(w0, w1) for w0, w1 in parts]
 
         log_d = keep.tile([P, BLOCKS, WIN], F32, name="log_d")
@@ -204,31 +205,32 @@ def tile_deepseekv4attention_pa_kernel(
             return acc
 
         pooled_t = [keep.tile([P, WIN], F32, name="pooled_t%d" % b) for b in range(BLOCKS)]
-        prod = [keep.tile([P, WIN, 2 * RATIO], F32, name="prod%d" % b) for b in range(BLOCKS)]
+        totals = [keep.tile([P, WIN], F32, name="total%d" % b) for b in range(BLOCKS)]
         LAST = BLOCKS - 1
 
         def lo_steps(b, acc):
-            out = [
-                lambda: tt(out=prod[b][:, 1:WIN, 0:4], in0=acc[:, 0 : BLOCK - RATIO].rearrange("p (w r) -> p w r", r=RATIO), in1=ex[b][:, 1:WIN, 0:4], op=ALU.mult),
-                lambda: tt(out=prod[b][:, 0:1, 0:4], in0=carry[b][:], in1=ex[b][:, 0:1, 0:4], op=ALU.mult),
+            n = WIN if b < LAST else WIN - 1
+            wins = slice(WIN * b + 1, WIN * b + 1 + n)
+            return [
+                lambda: tt(out=prod_all[:, wins, 0:4], in0=acc[:, 0 : RATIO * n].rearrange("p (w r) -> p w r", r=RATIO), in1=ex_all[:, wins, 0:4], op=ALU.mult),
             ]
-            if b < LAST:
-                out.append(lambda: nc.vector.tensor_copy(out=carry[b + 1][:, 0, :], in_=acc[:, BLOCK - RATIO : BLOCK]))
-            return out
 
         def hi_steps(b, w0, nw, acc):
             cols = slice(w0, w0 + nw)
-            total = pooled_t[b] if b == LAST else work.tile([P, WIN], F32, name="total")
+            wins = slice(WIN * b + w0, WIN * b + w0 + nw)
+            scaled = b == LAST and w0 >= PRE
+            total = pooled_t[b] if scaled else totals[b]
             out = [
-                lambda: tt(out=prod[b][:, cols, 4:8], in0=acc[:].rearrange("p (w r) -> p w r", r=RATIO), in1=ex[b][:, cols, 4:8], op=ALU.mult),
-                lambda: nc.vector.tensor_reduce(out=total[:, cols], in_=prod[b][:, cols, :], axis=AX.X, op=ALU.add),
+                lambda: tt(out=prod_all[:, wins, 4:8], in0=acc[:].rearrange("p (w r) -> p w r", r=RATIO), in1=ex_all[:, wins, 4:8], op=ALU.mult),
+                lambda: nc.vector.tensor_reduce(out=total[:, cols], in_=prod_all[:, wins, :], axis=AX.X, op=ALU.add),
             ]
-            if b < LAST:
+            if not scaled:
                 out.append(lambda: tt(out=pooled_t[b][:, cols], in0=total[:, cols], in1=recip[:, b, cols], op=ALU.mult))
             return out
 
         def prescale():
-            tt(out=ex[LAST][:], in0=ex[LAST][:], in1=recip[:, LAST, :].unsqueeze(2).to_broadcast([P, WIN, 8]), op=ALU.mult)
+            wins = slice(WIN * LAST + PRE, WIN * BLOCKS)
+            tt(out=ex_all[:, wins, :], in0=ex_all[:, wins, :], in1=recip[:, LAST, PRE:WIN].unsqueeze(2).to_broadcast([P, WIN - PRE, 8]), op=ALU.mult)
 
         pooled = [keep.tile([P, P], F32, name="pooled%d" % b) for b in range(BLOCKS)]
         turned = [keep.tile([P, HALF, 2], F32, name="turned%d" % b) for b in range(BLOCKS)]
@@ -281,34 +283,36 @@ def tile_deepseekv4attention_pa_kernel(
                 nc.scalar.activation(out=scrap[:], in_=zero[:], func=ACT.Exp)
             else:
                 exponent(b - 1)
-            weave(max_steps(b), sum_steps(b - 2, THIRDS) if b >= 2 else [])
+            tree = max_steps(b)
+            sums = sum_steps(b - 1, THIRDS) if b >= 1 else []
+            run(tree[0:3], sums[0:1], tree[3:4], sums[1:3])
 
-        late = []
+        his = {}
         for b in range(BLOCKS):
             lo_acc = kv_matmuls(b, 0, 0, WIN)
             if b == 0:
                 exponent(LAST)
-                run(sum_steps(LAST - 1, WHOLE))
             run(lo_steps(b, lo_acc))
+            if b == 0:
+                run(sum_steps(LAST, WHOLE))
+                reciprocals()
+            if b == 2:
+                run(his[0][2:3], his[1][2:3])
+                prescale()
             if b < LAST:
                 acc = kv_matmuls(b, 1, 0, WIN)
-                his = hi_steps(b, 0, WIN, acc)
-                if b == 0:
-                    run(his[0:1], sum_steps(LAST, WHOLE), his[1:2])
-                    reciprocals()
-                    late = late + his[2:3]
-                elif b == 1:
-                    run(his[0:2], late, his[2:3])
-                    prescale()
+                his[b] = hi_steps(b, 0, WIN, acc)
+                if b < 2:
+                    run(his[b][0:2])
                 else:
-                    run(his)
+                    run(his[b])
                     turn_round(0, False)
                     turn_round(1, False)
                     weave(rope_steps(0), rope_steps(1))
             else:
                 accs = [kv_matmuls(b, 1, w0, nw) for w0, nw in LAST_PIECES]
-                his = [hi_steps(b, w0, nw, acc) for (w0, nw), acc in zip(LAST_PIECES, accs)]
-                run(his[0][0:1], his[1][0:1], his[0][1:2], his[2][0:1], his[1][1:2], his[2][1:2])
+                p = [hi_steps(b, w0, nw, acc) for (w0, nw), acc in zip(LAST_PIECES, accs)]
+                run(p[0][0:1], p[1][0:1], p[0][1:2], p[2][0:1], p[0][2:3], p[1][1:2], p[2][1:2])
         turn_round(2, False)
         turn_round(3, True)
         run(rope_steps(2), rope_steps(3))

from contextlib import ExitStack
import concourse.mybir as mybir
from concourse.masks import make_identity

FLOPS = 2 * 2048 * 4096 * 512

F32 = mybir.dt.float32
BF16 = mybir.dt.bfloat16
I32 = mybir.dt.int32
U8 = mybir.dt.uint8
FP4 = mybir.dt.float4_e2m1fn_x4
ALU = mybir.AluOpType
ACT = mybir.ActivationFunctionType
AX = mybir.AxisListType

P = 128
PASSES = 8
BLOCKS = 4
BLOCK = 512
WIN = 128
RATIO = 4
HALF = 32
THETA = 10000.0
PITCH = 132
NEG = -1.0e30
HI_STEPS = 32768.0
TWO_PI = 6.283185307179586

LOADS = (
    ("s", "h0", 0, 2), ("s", "wg", 0, 8), ("c", "h0", 0, 2), ("c", "wg", 0, 2),
    ("s", "h0", 2, 8), ("c", "h0", 2, 4), ("c", "wg", 2, 8), ("c", "h0", 4, 8),
    ("s", "h1", 0, 8), ("c", "h1", 0, 4), ("c", "h1", 4, 8),
    ("s", "h2", 0, 8), ("c", "h2", 0, 4), ("c", "h2", 4, 8),
    ("s", "h3", 0, 8), ("c", "h3", 0, 4), ("c", "h3", 4, 8),
    ("s", "wk", 0, 8), ("c", "wk", 0, 8),
)
LAST_PIECES = ((0, 64), (64, 32), (96, 32))
PRE = 64


def tile_deepseekv4attention_pa_kernel(
    tc, hidden_words, hidden_scales, wkv_words, wkv_scales, wgate_words, wgate_scales, ape, out_0, out_1
):
    nc = tc.nc
    with ExitStack() as ctx:
        keep = ctx.enter_context(tc.tile_pool(name="keep", bufs=1))
        work = ctx.enter_context(tc.tile_pool(name="work", bufs=2))
        acc_pool = ctx.enter_context(tc.psum_pool(name="acc", bufs=6))
        tp_pool = ctx.enter_context(tc.psum_pool(name="tp", bufs=2))
        ctx.enter_context(tc.manual_schedule())

        source = {"wg": (wgate_words, wgate_scales, 0, 256), "wk": (wkv_words, wkv_scales, 0, 256)}
        for b in range(BLOCKS):
            source["h%d" % b] = (hidden_words, hidden_scales, BLOCK * b, BLOCK)
        codes = {}
        planes = {}

        ape_rows = keep.tile([2 * RATIO, P], BF16, name="ape_rows")
        nc.gpsimd.dma_start(out=ape_rows[:], in_=ape.rearrange("r (h f) -> (r h) f", h=2))

        plane_tiles = {}
        for kind, name, g0, g1 in LOADS:
            if kind == "s":
                cols = source[name][3]
                t = keep.tile([P, g1 - g0, cols], U8, name="%s_s%d" % (name, g0), align_bytes=64)
                nc.vector.memset(t[:].bitcast(I32), 0)
                plane_tiles[(name, g0)] = t
                for g in range(g0, g1):
                    planes[(name, g)] = t[:, g - g0, :]
        for kind, name, g0, g1 in LOADS:
            words, scales, c0, cols = source[name]
            if kind == "s":
                t = plane_tiles[(name, g0)]
                for q in range(4):
                    nc.sync.dma_start(
                        out=t[32 * q : 32 * q + 4, :, :].bitcast(I32),
                        in_=scales[g0:g1, 4 * q : 4 * q + 4, c0 : c0 + cols].rearrange("g r n -> r g n").bitcast(I32),
                    )
            else:
                t = keep.tile([P, g1 - g0, 2 * cols], U8, name="%s_c%d" % (name, g0), align_bytes=64)
                nc.sync.dma_start(
                    out=t[:].bitcast(I32),
                    in_=words[g0:g1, :, 2 * c0 : 2 * (c0 + cols)].rearrange("g p n -> p g n").bitcast(I32),
                )
                for g in range(g0, g1):
                    codes[(name, g)] = t[:, g - g0, :]

        zero = keep.tile([P, 1], F32, name="zero")
        nc.gpsimd.memset(zero[:], 0.0)
        wcol = keep.tile([P, BLOCKS], F32, name="wcol")
        nc.gpsimd.iota(wcol[:], pattern=[[WIN, BLOCKS]], base=0, channel_multiplier=1, allow_small_or_imprecise_dtypes=True)
        ape_pad = keep.tile([P, P], F32, name="ape_pad")
        nc.gpsimd.memset(ape_pad[:], 0.0)
        ident = keep.tile([P, P], F32, name="ident")
        make_identity(nc, ident[:])

        xg = [keep.tile([P, 2 * RATIO, PITCH], F32, name="xg%d" % b) for b in range(BLOCKS)]
        ex_all = keep.tile([P, BLOCKS * WIN, 2 * RATIO], F32, name="ex_all")
        prod_all = keep.tile([P, BLOCKS * WIN, 2 * RATIO], F32, name="prod_all")
        nc.gpsimd.memset(xg[0][:, 0:RATIO, 0:1], NEG)
        nc.vector.memset(prod_all[:, 0:1, 0:RATIO], 0.0)

        scrap = keep.tile([P, 1], F32, name="scrap")
        nc.scalar.activation(out=scrap[:], in_=zero[:], func=ACT.Sin)
        turn_hi = keep.tile([P, BLOCKS, HALF], F32, name="turn_hi")
        turn_lo = keep.tile([P, BLOCKS, HALF], F32, name="turn_lo")
        steps = [RATIO * THETA ** (-j / HALF) / TWO_PI for j in range(HALF)]
        for j in range(HALF):
            nc.scalar.mul(out=turn_hi[:, :, j], in_=wcol[:], mul=round(steps[j] * HI_STEPS) / HI_STEPS)
        for j in range(HALF):
            nc.scalar.mul(out=turn_lo[:, :, j], in_=wcol[:], mul=steps[j] - round(steps[j] * HI_STEPS) / HI_STEPS)

        nc.vector.tensor_copy(out=ape_pad[0 : 2 * RATIO, :], in_=ape_rows[:])
        ape_ps = tp_pool.tile([P, P], F32, name="ape_ps", tag="tp")
        nc.tensor.transpose(out=ape_ps[:], in_=ape_pad[:], identity=ident[:])
        ape_t = keep.tile([P, 2 * RATIO], F32, name="ape_t")
        nc.scalar.copy(out=ape_t[:], in_=ape_ps[:, 0 : 2 * RATIO])

        whole = keep.tile([P, BLOCKS, HALF], I32, name="whole")
        nc.vector.tensor_copy(out=whole[:], in_=turn_hi[:])
        frac = keep.tile([P, 2, BLOCKS, HALF], F32, name="frac")
        nc.vector.tensor_tensor(out=frac[:, 0], in0=turn_hi[:], in1=whole[:], op=ALU.subtract)
        nc.vector.tensor_tensor(out=frac[:, 0], in0=frac[:, 0], in1=turn_lo[:], op=ALU.add)
        nc.vector.tensor_scalar_add(out=frac[:, 1], in0=frac[:, 0], scalar1=0.25)
        wrap1 = keep.tile([P, 2 * BLOCKS * HALF], F32, name="wrap1")
        wrap2 = keep.tile([P, 2 * BLOCKS * HALF], F32, name="wrap2")
        flat = frac[:].rearrange("p a c j -> p (a c j)")
        nc.vector.scalar_tensor_tensor(out=wrap1[:], in0=flat, scalar=0.5, in1=flat, op0=ALU.is_gt, op1=ALU.subtract)
        nc.vector.scalar_tensor_tensor(out=wrap2[:], in0=wrap1[:], scalar=0.5, in1=wrap1[:], op0=ALU.is_gt, op1=ALU.subtract)
        sincos = keep.tile([P, 2, BLOCKS, HALF], F32, name="sincos")
        nc.scalar.activation(out=sincos[:].rearrange("p a c j -> p (a c j)"), in_=wrap2[:], func=ACT.Sin, scale=TWO_PI)

        def mx(acc, wname, half, b, g, col0, ncol):
            nc.tensor.matmul_mx(
                out=acc,
                lhsT=codes[(wname, g)][:, 256 * half : 256 * half + 256].bitcast(FP4),
                lhsT_scale=planes[(wname, g)][:, P * half : P * half + P],
                rhs=codes[("h%d" % b, g)][:, 2 * col0 : 2 * (col0 + ncol)].bitcast(FP4),
                rhs_scale=planes[("h%d" % b, g)][:, col0 : col0 + ncol],
                start=(g == 0),
                stop=(g == PASSES - 1),
            )

        def gate_matmuls(b):
            lo = acc_pool.tile([P, BLOCK], F32, name="gate_lo%d" % b, tag="acc")
            hi = acc_pool.tile([P, BLOCK], F32, name="gate_hi%d" % b, tag="acc")
            for g in range(PASSES):
                mx(lo[:], "wg", 0, b, g, 0, BLOCK)
                mx(hi[:], "wg", 1, b, g, 0, BLOCK)
            return lo, hi

        def add_offsets(b, banks):
            for half in range(2):
                shift = 1 - half
                for r in range(RATIO):
                    nc.scalar.activation(
                        out=xg[b][:, RATIO * half + r, shift : shift + WIN],
                        in_=banks[half][:, r:BLOCK:RATIO],
                        func=ACT.Identity,
                        bias=ape_t[:, 2 * r + half : 2 * r + half + 1],
                        scale=1.0,
                    )
            if b + 1 < BLOCKS:
                nc.gpsimd.tensor_copy(out=xg[b + 1][:, 0:RATIO, 0:1], in_=xg[b][:, 0:RATIO, WIN : WIN + 1])

        tt = nc.vector.tensor_tensor
        below = {}

        def max_steps(b):
            m4 = work.tile([P, 4, WIN], F32, name="m4")
            m2 = work.tile([P, 2, WIN], F32, name="m2")
            m1 = work.tile([P, WIN], F32, name="m1")
            dm = work.tile([P, 8, WIN], F32, name="dm")
            below[b] = dm
            return [
                lambda: tt(out=m4[:], in0=xg[b][:, 0:4, 0:WIN], in1=xg[b][:, 4:8, 0:WIN], op=ALU.max),
                lambda: tt(out=m2[:], in0=m4[:, 0:2, :], in1=m4[:, 2:4, :], op=ALU.max),
                lambda: tt(out=m1[:], in0=m2[:, 0, :], in1=m2[:, 1, :], op=ALU.max),
                lambda: tt(out=dm[:], in0=xg[b][:, :, 0:WIN], in1=m1[:].unsqueeze(1).to_broadcast([P, 8, WIN]), op=ALU.subtract),
            ]

        def exponent(b):
            for half in range(2):
                s = slice(RATIO * half, RATIO * half + RATIO)
                nc.scalar.activation(out=ex_all[:, WIN * b : WIN * (b + 1), s], in_=below[b][:, s, :].rearrange("p s w -> p w s"), func=ACT.Exp)

        denom = keep.tile([P, BLOCKS, WIN], F32, name="denom")

        def sum_steps(b, parts):
            def one(w0, w1):
                return lambda: nc.vector.tensor_reduce(out=denom[:, b, w0:w1], in_=ex_all[:, WIN * b + w0 : WIN * b + w1, :], axis=AX.X, op=ALU.add)
            return [one(w0, w1) for w0, w1 in parts]

        log_d = keep.tile([P, BLOCKS, WIN], F32, name="log_d")
        recip = keep.tile([P, BLOCKS, WIN], F32, name="recip")

        def reciprocals():
            nc.scalar.activation(out=log_d[:], in_=denom[:], func=ACT.Ln)
            nc.scalar.activation(out=recip[:], in_=log_d[:], func=ACT.Exp, scale=-1.0)

        def kv_matmuls(b, half, w0, nw):
            acc = acc_pool.tile([P, RATIO * nw], F32, name="kv%d_%d_%d" % (half, b, w0), tag="acc")
            for g in range(PASSES):
                mx(acc[:], "wk", half, b, g, RATIO * w0, RATIO * nw)
            return acc

        pooled_t = [keep.tile([P, WIN], F32, name="pooled_t%d" % b) for b in range(BLOCKS)]
        totals = [keep.tile([P, WIN], F32, name="total%d" % b) for b in range(BLOCKS)]
        LAST = BLOCKS - 1

        def lo_steps(b, acc):
            n = WIN if b < LAST else WIN - 1
            wins = slice(WIN * b + 1, WIN * b + 1 + n)
            return [
                lambda: tt(out=prod_all[:, wins, 0:4], in0=acc[:, 0 : RATIO * n].rearrange("p (w r) -> p w r", r=RATIO), in1=ex_all[:, wins, 0:4], op=ALU.mult),
            ]

        def hi_steps(b, w0, nw, acc):
            cols = slice(w0, w0 + nw)
            wins = slice(WIN * b + w0, WIN * b + w0 + nw)
            scaled = b == LAST and w0 >= PRE
            total = pooled_t[b] if scaled else totals[b]
            out = [
                lambda: tt(out=prod_all[:, wins, 4:8], in0=acc[:].rearrange("p (w r) -> p w r", r=RATIO), in1=ex_all[:, wins, 4:8], op=ALU.mult),
                lambda: nc.vector.tensor_reduce(out=total[:, cols], in_=prod_all[:, wins, :], axis=AX.X, op=ALU.add),
            ]
            if not scaled:
                out.append(lambda: tt(out=pooled_t[b][:, cols], in0=total[:, cols], in1=recip[:, b, cols], op=ALU.mult))
            return out

        def prescale():
            wins = slice(WIN * LAST + PRE, WIN * BLOCKS)
            tt(out=ex_all[:, wins, :], in0=ex_all[:, wins, :], in1=recip[:, LAST, PRE:WIN].unsqueeze(2).to_broadcast([P, WIN - PRE, 8]), op=ALU.mult)

        pooled = [keep.tile([P, P], F32, name="pooled%d" % b) for b in range(BLOCKS)]
        turned = [keep.tile([P, HALF, 2], F32, name="turned%d" % b) for b in range(BLOCKS)]
        rope_in = {}

        def turn_round(b, twice):
            ps = tp_pool.tile([P, P], F32, name="pooled_ps%d" % b, tag="tp")
            nc.tensor.transpose(out=ps[:], in_=pooled_t[b][:], identity=ident[:])
            rope_in[b] = pooled[b]
            if twice:
                ps2 = tp_pool.tile([P, P], F32, name="pooled_pt%d" % b, tag="tp")
                nc.tensor.transpose(out=ps2[:], in_=pooled_t[b][:], identity=ident[:])
                rope_in[b] = ps2
            nc.scalar.copy(out=pooled[b][:], in_=ps[:])
            rows = slice(WIN * b, WIN * (b + 1))
            nc.sync.dma_start(out=out_1[0, rows, :], in_=pooled[b][:])
            nc.sync.dma_start(out=out_0[0, rows, 0:64], in_=pooled[b][:, 0:64])

        def rope_steps(b):
            pairs = rope_in[b][:, 64:128].rearrange("p (j e) -> p j e", e=2)
            by_cos = work.tile([P, HALF, 2], F32, name="by_cos")
            by_sin = work.tile([P, HALF, 2], F32, name="by_sin")
            cos = sincos[:, 1, b, :].unsqueeze(2).to_broadcast([P, HALF, 2])
            sin = sincos[:, 0, b, :].unsqueeze(2).to_broadcast([P, HALF, 2])
            rows = slice(WIN * b, WIN * (b + 1))
            return [
                lambda: tt(out=by_cos[:], in0=pairs, in1=cos, op=ALU.mult),
                lambda: tt(out=by_sin[:], in0=pairs, in1=sin, op=ALU.mult),
                lambda: tt(out=turned[b][:, :, 0], in0=by_cos[:, :, 0], in1=by_sin[:, :, 1], op=ALU.subtract),
                lambda: tt(out=turned[b][:, :, 1], in0=by_cos[:, :, 1], in1=by_sin[:, :, 0], op=ALU.add),
                lambda: nc.sync.dma_start(out=out_0[0, rows, 64:128], in_=turned[b][:].rearrange("p j e -> p (j e)")),
            ]

        def run(*lists):
            for steps_ in lists:
                for step in steps_:
                    step()

        def weave(a, c):
            for i in range(max(len(a), len(c))):
                run(a[i : i + 1], c[i : i + 1])

        THIRDS = ((0, 48), (48, 96), (96, 128))
        WHOLE = ((0, WIN),)

        for b in range(BLOCKS):
            banks = gate_matmuls(b)
            add_offsets(b, banks)
            if b == 0:
                nc.scalar.activation(out=scrap[:], in_=zero[:], func=ACT.Exp)
            else:
                exponent(b - 1)
            tree = max_steps(b)
            sums = sum_steps(b - 1, THIRDS) if b >= 1 else []
            run(tree[0:3], sums[0:1], tree[3:4], sums[1:3])

        his = {}
        for b in range(BLOCKS):
            lo_acc = kv_matmuls(b, 0, 0, WIN)
            if b == 0:
                exponent(LAST)
            run(lo_steps(b, lo_acc))
            if b == 0:
                run(sum_steps(LAST, WHOLE))
                reciprocals()
            if b == 2:
                run(his[0][2:3], his[1][2:3])
                prescale()
            if b < LAST:
                acc = kv_matmuls(b, 1, 0, WIN)
                his[b] = hi_steps(b, 0, WIN, acc)
                if b < 2:
                    run(his[b][0:2])
                else:
                    run(his[b])
                    turn_round(0, False)
                    turn_round(1, False)
                    weave(rope_steps(0), rope_steps(1))
            else:
                accs = [kv_matmuls(b, 1, w0, nw) for w0, nw in LAST_PIECES]
                p = [hi_steps(b, w0, nw, acc) for (w0, nw), acc in zip(LAST_PIECES, accs)]
                run(p[0][0:1], p[1][0:1], p[0][1:2], p[2][0:1], p[0][2:3], p[1][1:2], p[2][1:2])
        turn_round(2, False)
        turn_round(3, True)
        run(rope_steps(2), rope_steps(3))
